import numpy as np
import ml_dtypes


def mxq(x, axis, fmt="e4m3"):
    dtype, down = {"e4m3": (ml_dtypes.float8_e4m3fn, 7), "e5m2": (ml_dtypes.float8_e5m2, 14)}[fmt]
    v = np.moveaxis(np.asarray(x, np.float32).astype(ml_dtypes.bfloat16).astype(np.float64), axis, -1)
    blocks = v.reshape(v.shape[:-1] + (-1, 32))
    amax = np.abs(blocks).max(-1, keepdims=True)
    byte = np.maximum(np.where(amax > 0, np.frexp(amax)[1] - 1 + 127, 0) - down, 1)
    scale = np.exp2(byte - 127.0)
    codes = (blocks / scale).astype(np.float32).astype(dtype).astype(np.float64)
    return np.moveaxis((codes * scale).reshape(v.shape), -1, axis)


WIDE = False


def mx_kscale(k):
    if not WIDE:
        return np.ones(k)
    levels = np.array([10, -10, 5, -5, 0])
    a = np.random.permutation(np.resize(levels, k // 512 * 4)).reshape(k // 512, 4)
    idx = np.arange(k)
    return np.exp2(a[idx // 512, idx % 128 // 32])


BF16 = ml_dtypes.bfloat16


def bf(x):
    return np.asarray(x, np.float32).astype(BF16)


def f64(x):
    return np.asarray(x).astype(np.float64)


E2M1 = np.array([0.0, 0.5, 1.0, 1.5, 2.0, 3.0, 4.0, 6.0, -0.0, -0.5, -1.0, -1.5, -2.0, -3.0, -4.0, -6.0])


def pack_weight(w, fmt):
    k, n = w.shape
    w = f64(bf(w)).reshape(k // 32, 32, n)
    amax = np.abs(w).max(1)
    if fmt == "e4m3":
        byte = np.frexp(amax)[1] - 1 + 127 - 7
    else:
        mant, ex = np.frexp(amax / 6.0)
        byte = np.where(mant > 0.5, ex, ex - 1) + 127
    byte = np.clip(np.where(amax > 0, byte, 1), 1, 254)
    scaled = (w * np.exp2(127.0 - byte)[:, None, :]).reshape(k, n).astype(np.float32)
    by_word = np.ascontiguousarray(scaled.reshape(k // 512, 128, 4, n).transpose(0, 1, 3, 2))
    if fmt == "e4m3":
        words = by_word.astype(ml_dtypes.float8_e4m3fn).view(np.uint8)
    else:
        c = by_word.astype(ml_dtypes.float4_e2m1fn).view(np.uint8) & 0xF
        words = c[..., 0::2] | (c[..., 1::2] << 4)
    return np.ascontiguousarray(words), np.ascontiguousarray(byte.astype(np.uint8).reshape(k // 512, 16, n))


def unpack_weight(words, scales, fmt):
    g, p, n, _ = words.shape
    if fmt == "e4m3":
        vals = np.ascontiguousarray(words).view(ml_dtypes.float8_e4m3fn).astype(np.float64)
    else:
        nib = np.empty((g, p, n, 4), np.uint8)
        nib[..., 0::2] = words & 0xF
        nib[..., 1::2] = words >> 4
        vals = E2M1[nib]
    vals = vals * np.repeat(np.exp2(scales.astype(np.float64) - 127.0), 8, axis=1)[..., None]
    return vals.transpose(0, 1, 3, 2).reshape(g * 512, n)

def pack4(w):
    words, scales = pack_weight(w, "e2m1")
    return words.reshape(words.shape[0], 128, -1), scales


def unpack4(words, scales):
    return unpack_weight(words.reshape(words.shape[0], 128, -1, 2), scales, "e2m1")


B, L, H = 4, 2048, 512
HH = H // 2
BASE = 10000.0


def rope_tables():
    inv_freq = 1.0 / BASE ** (np.arange(0, H, 2) / H)
    freqs = np.outer(np.arange(L), inv_freq)
    emb = np.concatenate([freqs, freqs], axis=-1)
    return np.cos(emb), np.sin(emb)


def rotate_half(x):
    x1, x2 = np.split(x, 2, axis=-1)
    return np.concatenate([-x2, x1], axis=-1)


def setup_inputs():
    sh = mx_kscale(H)[:HH]
    s = np.concatenate([sh, sh])
    cos, sin = rope_tables()
    hidden_states = bf(np.random.standard_normal((B, L, H)) * 0.2 * s)
    w = np.random.standard_normal((H, H)) * 0.5 / np.sqrt(H) / s[None, :]
    words, scales = pack4(np.ascontiguousarray(w.T))
    return {"hidden_states": hidden_states,
            "W_q_words": words, "W_q_scales": scales,
            "cos": bf(cos), "sin": bf(sin)}


def reference(hidden_states, W_q_words, W_q_scales, cos, sin):
    x = f64(hidden_states)
    h = x * f64(cos)[None, :, :] + rotate_half(x) * f64(sin)[None, :, :]
    return mxq(h, 2, "e4m3") @ unpack4(W_q_words, W_q_scales)

@@ -1,0 +1,176 @@
+from contextlib import ExitStack
+
+import concourse.mybir as mybir
+from concourse.masks import make_identity
+
+BF16 = mybir.dt.bfloat16
+F32 = mybir.dt.float32
+I32 = mybir.dt.int32
+U8 = mybir.dt.uint8
+U32 = mybir.dt.uint32
+FP8X4 = mybir.dt.float8_e4m3fn_x4
+FP4X4 = mybir.dt.float4_e2m1fn_x4
+MULT = mybir.AluOpType.mult
+
+B, L, H = 4, 2048, 512
+P = 128
+PACK = 4
+Q = H // PACK
+HALF_Q = Q // 2
+STEPS = L // P
+AHEAD = 3
+
+FLOPS = 2 * B * L * H * H
+
+
+def tile_denseattentiononehead_pa_t_kernel(
+    tc, hidden_states, W_q_words, W_q_scales, cos, sin, out
+):
+    nc = tc.nc
+    x_dram = hidden_states.rearrange("b (n p) j -> n p b j", p=P)
+    cos_dram = cos.rearrange("(n p) j -> n p j", p=P)
+    sin_dram = sin.rearrange("(n p) j -> n p j", p=P)
+    out_dram = out.rearrange("b (n p) o -> n p b o", p=P)
+
+    with ExitStack() as ctx:
+        consts = ctx.enter_context(tc.tile_pool(name="consts", bufs=1))
+        inputs = ctx.enter_context(tc.tile_pool(name="inputs", bufs=AHEAD + 1))
+        products = ctx.enter_context(tc.tile_pool(name="products", bufs=2))
+        quantised = ctx.enter_context(tc.tile_pool(name="quantised", bufs=2))
+        results = ctx.enter_context(tc.tile_pool(name="results", bufs=3))
+        psum_h = ctx.enter_context(tc.psum_pool(name="psum_h", bufs=B))
+        psum_out = ctx.enter_context(tc.psum_pool(name="psum_out", bufs=B))
+        ctx.enter_context(tc.manual_schedule())
+
+        identity = consts.tile([P, P], F32)
+        make_identity(nc, identity[:])
+
+        loaded, negated, multiplied, transposed, grouped, packed, projected = (
+            {}, {}, {}, {}, {}, {}, {},
+        )
+
+        def load(i):
+            cos_sb = inputs.tile([P, H], BF16)
+            nc.sync.dma_start(out=cos_sb[:], in_=cos_dram[i])
+            sin_sb = inputs.tile([P, H], BF16)
+            nc.sync.dma_start(out=sin_sb[:], in_=sin_dram[i])
+            x_sb = inputs.tile([P, B, H], BF16)
+            nc.sync.dma_start(out=x_sb[:], in_=x_dram[i])
+            loaded[i] = (x_sb, cos_sb, sin_sb)
+
+        def negate(i):
+            sin_sb = loaded[i][2]
+            minus_sin = inputs.tile([P, H // 2], BF16)
+            nc.scalar.mul(out=minus_sin[:], in_=sin_sb[:, 0 : H // 2], mul=-1.0)
+            negated[i] = minus_sin
+
+        def by_word_value(table):
+            view = table.rearrange("p (q t) -> p t q", t=PACK)
+            return view.unsqueeze(1).to_broadcast([P, B, PACK, view.shape[2]])
+
+        def multiply(i):
+            x_sb, cos_sb, sin_sb = loaded[i]
+            x_tq = x_sb[:].rearrange("p b (q t) -> p b t q", t=PACK)
+            x_cos = products.tile([P, B, PACK, Q], F32)
+            nc.vector.tensor_tensor(out=x_cos[:], in0=x_tq, in1=by_word_value(cos_sb[:]), op=MULT)
+            rot_sin = products.tile([P, B, PACK, Q], F32)
+            nc.vector.tensor_tensor(
+                out=rot_sin[:, :, :, 0:HALF_Q],
+                in0=x_tq[:, :, :, HALF_Q:Q],
+                in1=by_word_value(negated[i][:]),
+                op=MULT,
+            )
+            nc.vector.tensor_tensor(
+                out=rot_sin[:, :, :, HALF_Q:Q],
+                in0=x_tq[:, :, :, 0:HALF_Q],
+                in1=by_word_value(sin_sb[:, H // 2 : H]),
+                op=MULT,
+            )
+            multiplied[i] = (x_cos, rot_sin)
+
+        def transpose_and_add(i):
+            x_cos, rot_sin = multiplied[i]
+            transposed[i] = []
+            for b in range(B):
+                h_T = psum_h.tile([P, PACK, P], F32)
+                for t in range(PACK):
+                    nc.tensor.matmul(
+                        h_T[:, t, :], lhsT=x_cos[:, b, t, :], rhs=identity[:],
+                        is_transpose=True, start=True, stop=False,
+                    )
+                    nc.tensor.matmul(
+                        h_T[:, t, :], lhsT=rot_sin[:, b, t, :], rhs=identity[:],
+                        is_transpose=True, start=False, stop=True,
+                    )
+                transposed[i].append(h_T)
+
+        def regroup(i):
+            h_grouped = quantised.tile([P, B, P, PACK], BF16, align_bytes=64)
+            for b in range(B):
+                nc.scalar.copy(
+                    out=h_grouped[:, b, :, :], in_=transposed[i][b][:].rearrange("p t w -> p w t")
+                )
+            grouped[i] = h_grouped
+
+        def quantise(i):
+            h_codes = quantised.tile([P, B * P], U32, align_bytes=64)
+            h_scales = quantised.tile([P, B * P], U8, align_bytes=64)
+            nc.vector.quantize_mx(
+                out=h_codes[:].bitcast(FP8X4),
+                scales=h_scales[:],
+                in_=grouped[i][:].rearrange("p b w t -> p (b w t)"),
+            )
+            packed[i] = (h_codes, h_scales)
+
+        def project(i):
+            h_codes, h_scales = packed[i]
+            projected[i] = []
+            for b in range(B):
+                tokens = slice(b * P, (b + 1) * P)
+                acc = psum_out.tile([P, H], F32)
+                nc.tensor.matmul_mx(
+                    out=acc[:],
+                    lhsT=h_codes[:, tokens].bitcast(FP8X4),
+                    lhsT_scale=h_scales[:, tokens],
+                    rhs=w_words[:].bitcast(FP4X4),
+                    rhs_scale=w_scales[:],
+                    start=True,
+                    stop=True,
+                )
+                projected[i].append(acc)
+
+        def store(i):
+            out_sb = results.tile([P, B, H], F32)
+            for b in range(B):
+                nc.scalar.copy(out=out_sb[:, b, :], in_=projected[i][b][:])
+            nc.scalar.dma_start(out=out_dram[i], in_=out_sb[:])
+
+        load(0)
+
+        w_words = consts.tile([P, 2 * H], U8, align_bytes=64)
+        nc.sync.dma_start(out=w_words[:].bitcast(I32), in_=W_q_words[0].bitcast(I32))
+        w_scales = consts.tile([P, H], U8, align_bytes=64)
+        nc.vector.memset(w_scales[:].bitcast(I32), 0)
+        for quadrant in range(4):
+            nc.sync.dma_start(
+                out=w_scales[32 * quadrant : 32 * quadrant + 4, :].bitcast(I32),
+                in_=W_q_scales[0, 4 * quadrant : 4 * quadrant + 4, :].bitcast(I32),
+            )
+
+        for i in range(1, AHEAD):
+            load(i)
+        negate(0)
+
+        for i in range(STEPS + 1):
+            if i + AHEAD < STEPS:
+                load(i + AHEAD)
+            if i + 1 < STEPS:
+                negate(i + 1)
+            if i < STEPS:
+                multiply(i)
+                transpose_and_add(i)
+                regroup(i)
+            if i >= 1:
+                quantise(i - 1)
+                project(i - 1)
+                store(i - 1)

@@ -19,6 +19,8 @@ Q = H // PACK
 HALF_Q = Q // 2
 STEPS = L // P
 AHEAD = 3
+RUN = 2
+RUNS = B // RUN
 
 FLOPS = 2 * B * L * H * H
 
@@ -36,8 +38,8 @@ def tile_denseattentiononehead_pa_t_kernel(
         consts = ctx.enter_context(tc.tile_pool(name="consts", bufs=1))
         inputs = ctx.enter_context(tc.tile_pool(name="inputs", bufs=AHEAD + 1))
         products = ctx.enter_context(tc.tile_pool(name="products", bufs=2))
-        quantised = ctx.enter_context(tc.tile_pool(name="quantised", bufs=2))
-        results = ctx.enter_context(tc.tile_pool(name="results", bufs=3))
+        quantised = ctx.enter_context(tc.tile_pool(name="quantised", bufs=2 * RUNS))
+        results = ctx.enter_context(tc.tile_pool(name="results", bufs=3 * RUNS))
         psum_h = ctx.enter_context(tc.psum_pool(name="psum_h", bufs=B))
         psum_out = ctx.enter_context(tc.psum_pool(name="psum_out", bufs=B))
         ctx.enter_context(tc.manual_schedule())
@@ -88,10 +90,10 @@ def tile_denseattentiononehead_pa_t_kernel(
             )
             multiplied[i] = (x_cos, rot_sin)
 
-        def transpose_and_add(i):
+        def transpose_and_add(i, r):
             x_cos, rot_sin = multiplied[i]
-            transposed[i] = []
-            for b in range(B):
+            transposed[i, r] = []
+            for b in range(r * RUN, (r + 1) * RUN):
                 h_T = psum_h.tile([P, PACK, P], F32)
                 for t in range(PACK):
                     nc.tensor.matmul(
@@ -102,31 +104,32 @@ def tile_denseattentiononehead_pa_t_kernel(
                         h_T[:, t, :], lhsT=rot_sin[:, b, t, :], rhs=identity[:],
                         is_transpose=True, start=False, stop=True,
                     )
-                transposed[i].append(h_T)
+                transposed[i, r].append(h_T)
 
-        def regroup(i):
-            h_grouped = quantised.tile([P, B, P, PACK], BF16, align_bytes=64)
-            for b in range(B):
+        def regroup(i, r):
+            h_grouped = quantised.tile([P, RUN, P, PACK], BF16, align_bytes=64)
+            for k in range(RUN):
                 nc.scalar.copy(
-                    out=h_grouped[:, b, :, :], in_=transposed[i][b][:].rearrange("p t w -> p w t")
+                    out=h_grouped[:, k, :, :],
+                    in_=transposed[i, r][k][:].rearrange("p t w -> p w t"),
                 )
-            grouped[i] = h_grouped
+            grouped[i, r] = h_grouped
 
-        def quantise(i):
-            h_codes = quantised.tile([P, B * P], U32, align_bytes=64)
-            h_scales = quantised.tile([P, B * P], U8, align_bytes=64)
+        def quantise(i, r):
+            h_codes = quantised.tile([P, RUN * P], U32, align_bytes=64)
+            h_scales = quantised.tile([P, RUN * P], U8, align_bytes=64)
             nc.vector.quantize_mx(
                 out=h_codes[:].bitcast(FP8X4),
                 scales=h_scales[:],
-                in_=grouped[i][:].rearrange("p b w t -> p (b w t)"),
+                in_=grouped[i, r][:].rearrange("p k w t -> p (k w t)"),
             )
-            packed[i] = (h_codes, h_scales)
+            packed[i, r] = (h_codes, h_scales)
 
-        def project(i):
-            h_codes, h_scales = packed[i]
-            projected[i] = []
-            for b in range(B):
-                tokens = slice(b * P, (b + 1) * P)
+        def project(i, r):
+            h_codes, h_scales = packed[i, r]
+            projected[i, r] = []
+            for k in range(RUN):
+                tokens = slice(k * P, (k + 1) * P)
                 acc = psum_out.tile([P, H], F32)
                 nc.tensor.matmul_mx(
                     out=acc[:],
@@ -137,13 +140,13 @@ def tile_denseattentiononehead_pa_t_kernel(
                     start=True,
                     stop=True,
                 )
-                projected[i].append(acc)
+                projected[i, r].append(acc)
 
-        def store(i):
-            out_sb = results.tile([P, B, H], F32)
-            for b in range(B):
-                nc.scalar.copy(out=out_sb[:, b, :], in_=projected[i][b][:])
-            nc.scalar.dma_start(out=out_dram[i], in_=out_sb[:])
+        def store(i, r):
+            out_sb = results.tile([P, RUN, H], F32)
+            for k in range(RUN):
+                nc.scalar.copy(out=out_sb[:, k, :], in_=projected[i, r][k][:])
+            nc.scalar.dma_start(out=out_dram[i][:, r * RUN : (r + 1) * RUN, :], in_=out_sb[:])
 
         load(0)
 
@@ -168,9 +171,13 @@ def tile_denseattentiononehead_pa_t_kernel(
                 negate(i + 1)
             if i < STEPS:
                 multiply(i)
-                transpose_and_add(i)
-                regroup(i)
-            if i >= 1:
-                quantise(i - 1)
-                project(i - 1)
-                store(i - 1)
+            for r in range(RUNS):
+                if i >= 1:
+                    quantise(i - 1, r)
+            for r in range(RUNS):
+                if i < STEPS:
+                    transpose_and_add(i, r)
+                    regroup(i, r)
+                if i >= 1:
+                    project(i - 1, r)
+                    store(i - 1, r)

@@ -19,8 +19,7 @@ Q = H // PACK
 HALF_Q = Q // 2
 STEPS = L // P
 AHEAD = 3
-RUN = 2
-RUNS = B // RUN
+VISIT = 2
 
 FLOPS = 2 * B * L * H * H
 
@@ -38,8 +37,8 @@ def tile_denseattentiononehead_pa_t_kernel(
         consts = ctx.enter_context(tc.tile_pool(name="consts", bufs=1))
         inputs = ctx.enter_context(tc.tile_pool(name="inputs", bufs=AHEAD + 1))
         products = ctx.enter_context(tc.tile_pool(name="products", bufs=2))
-        quantised = ctx.enter_context(tc.tile_pool(name="quantised", bufs=2 * RUNS))
-        results = ctx.enter_context(tc.tile_pool(name="results", bufs=3 * RUNS))
+        quantised = ctx.enter_context(tc.tile_pool(name="quantised", bufs=2))
+        results = ctx.enter_context(tc.tile_pool(name="results", bufs=3))
         psum_h = ctx.enter_context(tc.psum_pool(name="psum_h", bufs=B))
         psum_out = ctx.enter_context(tc.psum_pool(name="psum_out", bufs=B))
         ctx.enter_context(tc.manual_schedule())
@@ -90,46 +89,47 @@ def tile_denseattentiononehead_pa_t_kernel(
             )
             multiplied[i] = (x_cos, rot_sin)
 
-        def transpose_and_add(i, r):
+        def transpose_and_add(i):
             x_cos, rot_sin = multiplied[i]
-            transposed[i, r] = []
-            for b in range(r * RUN, (r + 1) * RUN):
+            transposed[i] = []
+            for b in range(B):
                 h_T = psum_h.tile([P, PACK, P], F32)
-                for t in range(PACK):
-                    nc.tensor.matmul(
-                        h_T[:, t, :], lhsT=x_cos[:, b, t, :], rhs=identity[:],
-                        is_transpose=True, start=True, stop=False,
-                    )
-                    nc.tensor.matmul(
-                        h_T[:, t, :], lhsT=rot_sin[:, b, t, :], rhs=identity[:],
-                        is_transpose=True, start=False, stop=True,
-                    )
-                transposed[i, r].append(h_T)
+                transposed[i].append(h_T)
+            for first_t in range(0, PACK, VISIT):
+                for b in range(B):
+                    for t in range(first_t, first_t + VISIT):
+                        nc.tensor.matmul(
+                            transposed[i][b][:, t, :], lhsT=x_cos[:, b, t, :], rhs=identity[:],
+                            is_transpose=True, start=True, stop=False,
+                        )
+                        nc.tensor.matmul(
+                            transposed[i][b][:, t, :], lhsT=rot_sin[:, b, t, :], rhs=identity[:],
+                            is_transpose=True, start=False, stop=True,
+                        )
 
-        def regroup(i, r):
-            h_grouped = quantised.tile([P, RUN, P, PACK], BF16, align_bytes=64)
-            for k in range(RUN):
+        def regroup(i):
+            h_grouped = quantised.tile([P, B, P, PACK], BF16, align_bytes=64)
+            for b in range(B):
                 nc.scalar.copy(
-                    out=h_grouped[:, k, :, :],
-                    in_=transposed[i, r][k][:].rearrange("p t w -> p w t"),
+                    out=h_grouped[:, b, :, :], in_=transposed[i][b][:].rearrange("p t w -> p w t")
                 )
-            grouped[i, r] = h_grouped
+            grouped[i] = h_grouped
 
-        def quantise(i, r):
-            h_codes = quantised.tile([P, RUN * P], U32, align_bytes=64)
-            h_scales = quantised.tile([P, RUN * P], U8, align_bytes=64)
+        def quantise(i):
+            h_codes = quantised.tile([P, B * P], U32, align_bytes=64)
+            h_scales = quantised.tile([P, B * P], U8, align_bytes=64)
             nc.vector.quantize_mx(
                 out=h_codes[:].bitcast(FP8X4),
                 scales=h_scales[:],
-                in_=grouped[i, r][:].rearrange("p k w t -> p (k w t)"),
+                in_=grouped[i][:].rearrange("p b w t -> p (b w t)"),
             )
-            packed[i, r] = (h_codes, h_scales)
+            packed[i] = (h_codes, h_scales)
 
-        def project(i, r):
-            h_codes, h_scales = packed[i, r]
-            projected[i, r] = []
-            for k in range(RUN):
-                tokens = slice(k * P, (k + 1) * P)
+        def project(i):
+            h_codes, h_scales = packed[i]
+            projected[i] = []
+            for b in range(B):
+                tokens = slice(b * P, (b + 1) * P)
                 acc = psum_out.tile([P, H], F32)
                 nc.tensor.matmul_mx(
                     out=acc[:],
@@ -140,13 +140,13 @@ def tile_denseattentiononehead_pa_t_kernel(
                     start=True,
                     stop=True,
                 )
-                projected[i, r].append(acc)
+                projected[i].append(acc)
 
-        def store(i, r):
-            out_sb = results.tile([P, RUN, H], F32)
-            for k in range(RUN):
-                nc.scalar.copy(out=out_sb[:, k, :], in_=projected[i, r][k][:])
-            nc.scalar.dma_start(out=out_dram[i][:, r * RUN : (r + 1) * RUN, :], in_=out_sb[:])
+        def store(i):
+            out_sb = results.tile([P, B, H], F32)
+            for b in range(B):
+                nc.scalar.copy(out=out_sb[:, b, :], in_=projected[i][b][:])
+            nc.scalar.dma_start(out=out_dram[i], in_=out_sb[:])
 
         load(0)
 
@@ -171,13 +171,9 @@ def tile_denseattentiononehead_pa_t_kernel(
                 negate(i + 1)
             if i < STEPS:
                 multiply(i)
-            for r in range(RUNS):
-                if i >= 1:
-                    quantise(i - 1, r)
-            for r in range(RUNS):
-                if i < STEPS:
-                    transpose_and_add(i, r)
-                    regroup(i, r)
-                if i >= 1:
-                    project(i - 1, r)
-                    store(i - 1, r)
+                transpose_and_add(i)
+                regroup(i)
+            if i >= 1:
+                quantise(i - 1)
+                project(i - 1)
+                store(i - 1)

@@ -19,7 +19,8 @@ Q = H // PACK
 HALF_Q = Q // 2
 STEPS = L // P
 AHEAD = 3
-VISIT = 2
+HALVES = ((0, 1), (2, 3))
+PASSES = (1, 1, 1, 1)
 
 FLOPS = 2 * B * L * H * H
 
@@ -36,8 +37,8 @@ def tile_denseattentiononehead_pa_t_kernel(
     with ExitStack() as ctx:
         consts = ctx.enter_context(tc.tile_pool(name="consts", bufs=1))
         inputs = ctx.enter_context(tc.tile_pool(name="inputs", bufs=AHEAD + 1))
-        products = ctx.enter_context(tc.tile_pool(name="products", bufs=2))
-        quantised = ctx.enter_context(tc.tile_pool(name="quantised", bufs=2))
+        products = ctx.enter_context(tc.tile_pool(name="products", bufs=3))
+        quantised = ctx.enter_context(tc.tile_pool(name="quantised", bufs=3))
         results = ctx.enter_context(tc.tile_pool(name="results", bufs=3))
         psum_h = ctx.enter_context(tc.psum_pool(name="psum_h", bufs=B))
         psum_out = ctx.enter_context(tc.psum_pool(name="psum_out", bufs=B))
@@ -46,8 +47,8 @@ def tile_denseattentiononehead_pa_t_kernel(
         identity = consts.tile([P, P], F32)
         make_identity(nc, identity[:])
 
-        loaded, negated, multiplied, transposed, grouped, packed, projected = (
-            {}, {}, {}, {}, {}, {}, {},
+        loaded, negated, multiplied, transposed, grouped, packed, projected, results_of = (
+            {}, {}, {}, {}, {}, {}, {}, {},
         )
 
         def load(i):
@@ -89,31 +90,30 @@ def tile_denseattentiononehead_pa_t_kernel(
             )
             multiplied[i] = (x_cos, rot_sin)
 
-        def transpose_and_add(i):
+        def transpose_and_add(i, batches):
             x_cos, rot_sin = multiplied[i]
-            transposed[i] = []
-            for b in range(B):
+            for b in batches:
                 h_T = psum_h.tile([P, PACK, P], F32)
-                transposed[i].append(h_T)
-            for first_t in range(0, PACK, VISIT):
-                for b in range(B):
-                    for t in range(first_t, first_t + VISIT):
-                        nc.tensor.matmul(
-                            transposed[i][b][:, t, :], lhsT=x_cos[:, b, t, :], rhs=identity[:],
-                            is_transpose=True, start=True, stop=False,
-                        )
-                        nc.tensor.matmul(
-                            transposed[i][b][:, t, :], lhsT=rot_sin[:, b, t, :], rhs=identity[:],
-                            is_transpose=True, start=False, stop=True,
-                        )
+                transposed[(i, b)] = h_T
+                for t in range(PACK):
+                    nc.tensor.matmul(
+                        h_T[:, t, :], lhsT=x_cos[:, b, t, :], rhs=identity[:],
+                        is_transpose=True, start=True, stop=False,
+                    )
+                    nc.tensor.matmul(
+                        h_T[:, t, :], lhsT=rot_sin[:, b, t, :], rhs=identity[:],
+                        is_transpose=True, start=False, stop=True,
+                    )
 
-        def regroup(i):
-            h_grouped = quantised.tile([P, B, P, PACK], BF16, align_bytes=64)
-            for b in range(B):
+        def regroup(i, batches):
+            if i not in grouped:
+                h_grouped = quantised.tile([P, B, P, PACK], BF16, align_bytes=64)
+                grouped[i] = h_grouped
+            for b in batches:
                 nc.scalar.copy(
-                    out=h_grouped[:, b, :, :], in_=transposed[i][b][:].rearrange("p t w -> p w t")
+                    out=grouped[i][:, b, :, :],
+                    in_=transposed[(i, b)][:].rearrange("p t w -> p w t"),
                 )
-            grouped[i] = h_grouped
 
         def quantise(i):
             h_codes = quantised.tile([P, B * P], U32, align_bytes=64)
@@ -125,28 +125,32 @@ def tile_denseattentiononehead_pa_t_kernel(
             )
             packed[i] = (h_codes, h_scales)
 
-        def project(i):
+        def project(i, batches):
             h_codes, h_scales = packed[i]
-            projected[i] = []
-            for b in range(B):
+            for b in batches:
                 tokens = slice(b * P, (b + 1) * P)
                 acc = psum_out.tile([P, H], F32)
-                nc.tensor.matmul_mx(
-                    out=acc[:],
-                    lhsT=h_codes[:, tokens].bitcast(FP8X4),
-                    lhsT_scale=h_scales[:, tokens],
-                    rhs=w_words[:].bitcast(FP4X4),
-                    rhs_scale=w_scales[:],
-                    start=True,
-                    stop=True,
-                )
-                projected[i].append(acc)
+                for again in range(PASSES[b]):
+                    nc.tensor.matmul_mx(
+                        out=acc[:],
+                        lhsT=h_codes[:, tokens].bitcast(FP8X4),
+                        lhsT_scale=h_scales[:, tokens],
+                        rhs=w_words[:].bitcast(FP4X4),
+                        rhs_scale=w_scales[:],
+                        start=True,
+                        stop=True,
+                    )
+                projected[(i, b)] = acc
+
+        def copy_out(i, batches):
+            if i not in results_of:
+                out_sb = results.tile([P, B, H], F32)
+                results_of[i] = out_sb
+            for b in batches:
+                nc.scalar.copy(out=results_of[i][:, b, :], in_=projected[(i, b)][:])
 
         def store(i):
-            out_sb = results.tile([P, B, H], F32)
-            for b in range(B):
-                nc.scalar.copy(out=out_sb[:, b, :], in_=projected[i][b][:])
-            nc.scalar.dma_start(out=out_dram[i], in_=out_sb[:])
+            nc.scalar.dma_start(out=out_dram[i], in_=results_of[i][:])
 
         load(0)
 
@@ -164,16 +168,21 @@ def tile_denseattentiononehead_pa_t_kernel(
             load(i)
         negate(0)
 
-        for i in range(STEPS + 1):
-            if i + AHEAD < STEPS:
-                load(i + AHEAD)
-            if i + 1 < STEPS:
-                negate(i + 1)
-            if i < STEPS:
-                multiply(i)
-                transpose_and_add(i)
-                regroup(i)
-            if i >= 1:
-                quantise(i - 1)
-                project(i - 1)
-                store(i - 1)
+        for s in range(STEPS + 2):
+            if AHEAD <= s + AHEAD < STEPS:
+                load(s + AHEAD)
+            if s + 1 < STEPS:
+                negate(s + 1)
+            if 0 <= s - 2:
+                quantise(s - 2)
+            if s < STEPS:
+                multiply(s)
+            for batches in HALVES:
+                if 0 <= s - 1 < STEPS:
+                    transpose_and_add(s - 1, batches)
+                    regroup(s - 1, batches)
+                if 0 <= s - 2:
+                    project(s - 2, batches)
+                    copy_out(s - 2, batches)
+            if 0 <= s - 2:
+                store(s - 2)

@@ -168,21 +168,21 @@ def tile_denseattentiononehead_pa_t_kernel(
             load(i)
         negate(0)
 
-        for s in range(STEPS + 2):
+        for s in range(STEPS + 3):
             if AHEAD <= s + AHEAD < STEPS:
                 load(s + AHEAD)
             if s + 1 < STEPS:
                 negate(s + 1)
-            if 0 <= s - 2:
-                quantise(s - 2)
+            if 0 <= s - 3:
+                quantise(s - 3)
             if s < STEPS:
                 multiply(s)
             for batches in HALVES:
                 if 0 <= s - 1 < STEPS:
                     transpose_and_add(s - 1, batches)
                     regroup(s - 1, batches)
-                if 0 <= s - 2:
-                    project(s - 2, batches)
-                    copy_out(s - 2, batches)
-            if 0 <= s - 2:
-                store(s - 2)
+                if 0 <= s - 3:
+                    project(s - 3, batches)
+                    copy_out(s - 3, batches)
+            if 0 <= s - 3:
+                store(s - 3)

@@ -18,9 +18,7 @@ PACK = 4
 Q = H // PACK
 HALF_Q = Q // 2
 STEPS = L // P
-AHEAD = 3
-HALVES = ((0, 1), (2, 3))
-PASSES = (1, 1, 1, 1)
+CHUNKS = (1, 1, 2, 4, 4, 4)
 
 FLOPS = 2 * B * L * H * H
 
@@ -29,17 +27,17 @@ def tile_denseattentiononehead_pa_t_kernel(
     tc, hidden_states, W_q_words, W_q_scales, cos, sin, out
 ):
     nc = tc.nc
-    x_dram = hidden_states.rearrange("b (n p) j -> n p b j", p=P)
-    cos_dram = cos.rearrange("(n p) j -> n p j", p=P)
-    sin_dram = sin.rearrange("(n p) j -> n p j", p=P)
-    out_dram = out.rearrange("b (n p) o -> n p b o", p=P)
+    x_dram = hidden_states.rearrange("b (p n) j -> p b n j", n=STEPS)
+    cos_dram = cos.rearrange("(p n) j -> p n j", n=STEPS)
+    sin_dram = sin.rearrange("(p n) j -> p n j", n=STEPS)
+    out_dram = out.rearrange("b (p n) o -> n p b o", n=STEPS)
 
     with ExitStack() as ctx:
         consts = ctx.enter_context(tc.tile_pool(name="consts", bufs=1))
-        inputs = ctx.enter_context(tc.tile_pool(name="inputs", bufs=AHEAD + 1))
+        inputs = ctx.enter_context(tc.tile_pool(name="inputs", bufs=1))
         products = ctx.enter_context(tc.tile_pool(name="products", bufs=3))
         quantised = ctx.enter_context(tc.tile_pool(name="quantised", bufs=3))
-        results = ctx.enter_context(tc.tile_pool(name="results", bufs=3))
+        results = ctx.enter_context(tc.tile_pool(name="results", bufs=4))
         psum_h = ctx.enter_context(tc.psum_pool(name="psum_h", bufs=B))
         psum_out = ctx.enter_context(tc.psum_pool(name="psum_out", bufs=B))
         ctx.enter_context(tc.manual_schedule())
@@ -47,39 +45,48 @@ def tile_denseattentiononehead_pa_t_kernel(
         identity = consts.tile([P, P], F32)
         make_identity(nc, identity[:])
 
-        loaded, negated, multiplied, transposed, grouped, packed, projected, results_of = (
+        loaded, negated, multiplied, transposed, grouped, packed, projected, chunk_of = (
             {}, {}, {}, {}, {}, {}, {}, {},
         )
 
-        def load(i):
-            cos_sb = inputs.tile([P, H], BF16)
-            nc.sync.dma_start(out=cos_sb[:], in_=cos_dram[i])
-            sin_sb = inputs.tile([P, H], BF16)
-            nc.sync.dma_start(out=sin_sb[:], in_=sin_dram[i])
-            x_sb = inputs.tile([P, B, H], BF16)
-            nc.sync.dma_start(out=x_sb[:], in_=x_dram[i])
-            loaded[i] = (x_sb, cos_sb, sin_sb)
+        def load(chunk, first, steps):
+            rows = slice(first, first + steps)
+            cos_sb = inputs.tile([P, steps, H], BF16, name="cos%d" % chunk)
+            nc.sync.dma_start(out=cos_sb[:], in_=cos_dram[:, rows, :])
+            sin_sb = inputs.tile([P, steps, H], BF16, name="sin%d" % chunk)
+            nc.sync.dma_start(out=sin_sb[:], in_=sin_dram[:, rows, :])
+            x_sb = inputs.tile([P, B, steps, H], BF16, name="x%d" % chunk)
+            nc.sync.dma_start(out=x_sb[:], in_=x_dram[:, :, rows, :])
+            minus_sin = inputs.tile([P, steps, H // 2], BF16, name="minus_sin%d" % chunk)
+            for k in range(steps):
+                loaded[first + k] = (x_sb[:, :, k, :], cos_sb[:, k, :], sin_sb[:, k, :])
+                negated[first + k] = minus_sin[:, k, :]
+            chunk_of[first] = (sin_sb, minus_sin)
 
         def negate(i):
-            sin_sb = loaded[i][2]
-            minus_sin = inputs.tile([P, H // 2], BF16)
-            nc.scalar.mul(out=minus_sin[:], in_=sin_sb[:, 0 : H // 2], mul=-1.0)
-            negated[i] = minus_sin
+            if i in chunk_of:
+                sin_sb, minus_sin = chunk_of[i]
+                nc.scalar.mul(out=minus_sin[:], in_=sin_sb[:, :, 0 : H // 2], mul=-1.0)
 
         def by_word_value(table):
             view = table.rearrange("p (q t) -> p t q", t=PACK)
             return view.unsqueeze(1).to_broadcast([P, B, PACK, view.shape[2]])
 
-        def multiply(i):
+        def multiply_by_cos(i):
             x_sb, cos_sb, sin_sb = loaded[i]
-            x_tq = x_sb[:].rearrange("p b (q t) -> p b t q", t=PACK)
+            x_tq = x_sb.rearrange("p b (q t) -> p b t q", t=PACK)
             x_cos = products.tile([P, B, PACK, Q], F32)
-            nc.vector.tensor_tensor(out=x_cos[:], in0=x_tq, in1=by_word_value(cos_sb[:]), op=MULT)
+            nc.vector.tensor_tensor(out=x_cos[:], in0=x_tq, in1=by_word_value(cos_sb), op=MULT)
+            return x_cos
+
+        def multiply_by_sin(i, x_cos):
+            x_sb, cos_sb, sin_sb = loaded[i]
+            x_tq = x_sb.rearrange("p b (q t) -> p b t q", t=PACK)
             rot_sin = products.tile([P, B, PACK, Q], F32)
             nc.vector.tensor_tensor(
                 out=rot_sin[:, :, :, 0:HALF_Q],
                 in0=x_tq[:, :, :, HALF_Q:Q],
-                in1=by_word_value(negated[i][:]),
+                in1=by_word_value(negated[i]),
                 op=MULT,
             )
             nc.vector.tensor_tensor(
@@ -90,9 +97,9 @@ def tile_denseattentiononehead_pa_t_kernel(
             )
             multiplied[i] = (x_cos, rot_sin)
 
-        def transpose_and_add(i, batches):
+        def transpose_and_add(i):
             x_cos, rot_sin = multiplied[i]
-            for b in batches:
+            for b in range(B):
                 h_T = psum_h.tile([P, PACK, P], F32)
                 transposed[(i, b)] = h_T
                 for t in range(PACK):
@@ -105,15 +112,14 @@ def tile_denseattentiononehead_pa_t_kernel(
                         is_transpose=True, start=False, stop=True,
                     )
 
-        def regroup(i, batches):
-            if i not in grouped:
-                h_grouped = quantised.tile([P, B, P, PACK], BF16, align_bytes=64)
-                grouped[i] = h_grouped
-            for b in batches:
+        def regroup(i):
+            h_grouped = quantised.tile([P, B, P, PACK], BF16, align_bytes=64)
+            for b in range(B):
                 nc.scalar.copy(
-                    out=grouped[i][:, b, :, :],
+                    out=h_grouped[:, b, :, :],
                     in_=transposed[(i, b)][:].rearrange("p t w -> p w t"),
                 )
+            grouped[i] = h_grouped
 
         def quantise(i):
             h_codes = quantised.tile([P, B * P], U32, align_bytes=64)
@@ -125,34 +131,32 @@ def tile_denseattentiononehead_pa_t_kernel(
             )
             packed[i] = (h_codes, h_scales)
 
-        def project(i, batches):
+        def project(i):
             h_codes, h_scales = packed[i]
-            for b in batches:
+            for b in range(B):
                 tokens = slice(b * P, (b + 1) * P)
                 acc = psum_out.tile([P, H], F32)
-                for again in range(PASSES[b]):
-                    nc.tensor.matmul_mx(
-                        out=acc[:],
-                        lhsT=h_codes[:, tokens].bitcast(FP8X4),
-                        lhsT_scale=h_scales[:, tokens],
-                        rhs=w_words[:].bitcast(FP4X4),
-                        rhs_scale=w_scales[:],
-                        start=True,
-                        stop=True,
-                    )
+                nc.tensor.matmul_mx(
+                    out=acc[:],
+                    lhsT=h_codes[:, tokens].bitcast(FP8X4),
+                    lhsT_scale=h_scales[:, tokens],
+                    rhs=w_words[:].bitcast(FP4X4),
+                    rhs_scale=w_scales[:],
+                    start=True,
+                    stop=True,
+                )
                 projected[(i, b)] = acc
 
-        def copy_out(i, batches):
-            if i not in results_of:
-                out_sb = results.tile([P, B, H], F32)
-                results_of[i] = out_sb
-            for b in batches:
-                nc.scalar.copy(out=results_of[i][:, b, :], in_=projected[(i, b)][:])
+        def copy_out(i, vector_helps):
+            out_sb = results.tile([P, B, H], F32)
+            for b in range(B):
+                if vector_helps and b % 2 == 1:
+                    nc.vector.tensor_copy(out=out_sb[:, b, :], in_=projected[(i, b)][:])
+                else:
+                    nc.scalar.copy(out=out_sb[:, b, :], in_=projected[(i, b)][:])
+            return out_sb
 
-        def store(i):
-            nc.scalar.dma_start(out=out_dram[i], in_=results_of[i][:])
-
-        load(0)
+        load(0, 0, CHUNKS[0])
 
         w_words = consts.tile([P, 2 * H], U8, align_bytes=64)
         nc.sync.dma_start(out=w_words[:].bitcast(I32), in_=W_q_words[0].bitcast(I32))
@@ -164,25 +168,32 @@ def tile_denseattentiononehead_pa_t_kernel(
                 in_=W_q_scales[0, 4 * quadrant : 4 * quadrant + 4, :].bitcast(I32),
             )
 
-        for i in range(1, AHEAD):
-            load(i)
+        for chunk in range(1, len(CHUNKS)):
+            load(chunk, sum(CHUNKS[:chunk]), CHUNKS[chunk])
         negate(0)
 
-        for s in range(STEPS + 3):
-            if AHEAD <= s + AHEAD < STEPS:
-                load(s + AHEAD)
-            if s + 1 < STEPS:
-                negate(s + 1)
-            if 0 <= s - 3:
-                quantise(s - 3)
-            if s < STEPS:
-                multiply(s)
-            for batches in HALVES:
-                if 0 <= s - 1 < STEPS:
-                    transpose_and_add(s - 1, batches)
-                    regroup(s - 1, batches)
-                if 0 <= s - 3:
-                    project(s - 3, batches)
-                    copy_out(s - 3, batches)
-            if 0 <= s - 3:
-                store(s - 3)
+        for s in range(STEPS):
+            negate(s + 1)
+            x_cos = multiply_by_cos(s)
+            if 0 <= s - 2:
+                quantise(s - 2)
+            multiply_by_sin(s, x_cos)
+            if 0 <= s - 1:
+                transpose_and_add(s - 1)
+                regroup(s - 1)
+            if 0 <= s - 2:
+                project(s - 2)
+                out_sb = copy_out(s - 2, False)
+                nc.sync.dma_start(out=out_dram[s - 2], in_=out_sb[:])
+
+        quantise(STEPS - 2)
+        transpose_and_add(STEPS - 1)
+        regroup(STEPS - 1)
+        project(STEPS - 2)
+        quantise(STEPS - 1)
+        out_sb = copy_out(STEPS - 2, True)
+        nc.sync.dma_start(out=out_dram[STEPS - 2], in_=out_sb[:])
+        project(STEPS - 1)
+        out_sb = copy_out(STEPS - 1, True)
+        for b in range(B):
+            nc.sync.dma_start(out=out_dram[STEPS - 1][:, b, :], in_=out_sb[:, b, :])

@@ -45,8 +45,8 @@ def tile_denseattentiononehead_pa_t_kernel(
         identity = consts.tile([P, P], F32)
         make_identity(nc, identity[:])
 
-        loaded, negated, multiplied, transposed, grouped, packed, projected, chunk_of = (
-            {}, {}, {}, {}, {}, {}, {}, {},
+        loaded, multiplied, transposed, grouped, packed, projected, chunk_of = (
+            {}, {}, {}, {}, {}, {}, {},
         )
 
         def load(chunk, first, steps):
@@ -54,19 +54,19 @@ def tile_denseattentiononehead_pa_t_kernel(
             cos_sb = inputs.tile([P, steps, H], BF16, name="cos%d" % chunk)
             nc.sync.dma_start(out=cos_sb[:], in_=cos_dram[:, rows, :])
             sin_sb = inputs.tile([P, steps, H], BF16, name="sin%d" % chunk)
-            nc.sync.dma_start(out=sin_sb[:], in_=sin_dram[:, rows, :])
+            nc.sync.dma_start(out=sin_sb[:, :, 0 : H // 2], in_=sin_dram[:, rows, H // 2 : H])
+            sin_low = inputs.tile([P, steps, H // 2], BF16, name="sin_low%d" % chunk)
+            nc.sync.dma_start(out=sin_low[:], in_=sin_dram[:, rows, 0 : H // 2])
             x_sb = inputs.tile([P, B, steps, H], BF16, name="x%d" % chunk)
             nc.sync.dma_start(out=x_sb[:], in_=x_dram[:, :, rows, :])
-            minus_sin = inputs.tile([P, steps, H // 2], BF16, name="minus_sin%d" % chunk)
             for k in range(steps):
                 loaded[first + k] = (x_sb[:, :, k, :], cos_sb[:, k, :], sin_sb[:, k, :])
-                negated[first + k] = minus_sin[:, k, :]
-            chunk_of[first] = (sin_sb, minus_sin)
+            chunk_of[first] = (sin_sb, sin_low)
 
         def negate(i):
             if i in chunk_of:
-                sin_sb, minus_sin = chunk_of[i]
-                nc.scalar.mul(out=minus_sin[:], in_=sin_sb[:, :, 0 : H // 2], mul=-1.0)
+                sin_sb, sin_low = chunk_of[i]
+                nc.scalar.mul(out=sin_sb[:, :, H // 2 : H], in_=sin_low[:], mul=-1.0)
 
         def by_word_value(table):
             view = table.rearrange("p (q t) -> p t q", t=PACK)
@@ -81,18 +81,13 @@ def tile_denseattentiononehead_pa_t_kernel(
 
         def multiply_by_sin(i, x_cos):
             x_sb, cos_sb, sin_sb = loaded[i]
-            x_tq = x_sb.rearrange("p b (q t) -> p b t q", t=PACK)
             rot_sin = products.tile([P, B, PACK, Q], F32)
             nc.vector.tensor_tensor(
-                out=rot_sin[:, :, :, 0:HALF_Q],
-                in0=x_tq[:, :, :, HALF_Q:Q],
-                in1=by_word_value(negated[i]),
-                op=MULT,
-            )
-            nc.vector.tensor_tensor(
-                out=rot_sin[:, :, :, HALF_Q:Q],
-                in0=x_tq[:, :, :, 0:HALF_Q],
-                in1=by_word_value(sin_sb[:, H // 2 : H]),
+                out=rot_sin[:].rearrange("p b t (h q) -> p b t h q", h=2)[:, :, :, ::-1, :],
+                in0=x_sb.rearrange("p b (h q t) -> p b t h q", h=2, t=PACK),
+                in1=sin_sb.rearrange("p (h q t) -> p t h q", h=2, t=PACK)
+                .unsqueeze(1)
+                .to_broadcast([P, B, PACK, 2, HALF_Q]),
                 op=MULT,
             )
             multiplied[i] = (x_cos, rot_sin)

@@ -19,6 +19,8 @@ Q = H // PACK
 HALF_Q = Q // 2
 STEPS = L // P
 CHUNKS = (1, 1, 2, 4, 4, 4)
+ALL = slice(0, B)
+HALVES = (slice(0, B // 2), slice(B // 2, B))
 
 FLOPS = 2 * B * L * H * H
 
@@ -51,14 +53,17 @@ def tile_denseattentiononehead_pa_t_kernel(
 
         def load(chunk, first, steps):
             rows = slice(first, first + steps)
-            cos_sb = inputs.tile([P, steps, H], BF16, name="cos%d" % chunk)
-            nc.sync.dma_start(out=cos_sb[:], in_=cos_dram[:, rows, :])
-            sin_sb = inputs.tile([P, steps, H], BF16, name="sin%d" % chunk)
-            nc.sync.dma_start(out=sin_sb[:, :, 0 : H // 2], in_=sin_dram[:, rows, H // 2 : H])
-            sin_low = inputs.tile([P, steps, H // 2], BF16, name="sin_low%d" % chunk)
-            nc.sync.dma_start(out=sin_low[:], in_=sin_dram[:, rows, 0 : H // 2])
             x_sb = inputs.tile([P, B, steps, H], BF16, name="x%d" % chunk)
-            nc.sync.dma_start(out=x_sb[:], in_=x_dram[:, :, rows, :])
+            cos_sb = inputs.tile([P, steps, H], BF16, name="cos%d" % chunk)
+            sin_sb = inputs.tile([P, steps, H], BF16, name="sin%d" % chunk)
+            sin_low = inputs.tile([P, steps, H // 2], BF16, name="sin_low%d" % chunk)
+            early = B // 2 if chunk == 0 else B
+            nc.sync.dma_start(out=x_sb[:, 0:early], in_=x_dram[:, 0:early, rows, :])
+            nc.sync.dma_start(out=cos_sb[:], in_=cos_dram[:, rows, :])
+            nc.sync.dma_start(out=sin_low[:], in_=sin_dram[:, rows, 0 : H // 2])
+            nc.sync.dma_start(out=sin_sb[:, :, 0 : H // 2], in_=sin_dram[:, rows, H // 2 : H])
+            if early < B:
+                nc.sync.dma_start(out=x_sb[:, early:B], in_=x_dram[:, early:B, rows, :])
             for k in range(steps):
                 loaded[first + k] = (x_sb[:, :, k, :], cos_sb[:, k, :], sin_sb[:, k, :])
             chunk_of[first] = (sin_sb, sin_low)
@@ -68,29 +73,29 @@ def tile_denseattentiononehead_pa_t_kernel(
                 sin_sb, sin_low = chunk_of[i]
                 nc.scalar.mul(out=sin_sb[:, :, H // 2 : H], in_=sin_low[:], mul=-1.0)
 
-        def by_word_value(table):
-            view = table.rearrange("p (q t) -> p t q", t=PACK)
-            return view.unsqueeze(1).to_broadcast([P, B, PACK, view.shape[2]])
-
-        def multiply_by_cos(i):
+        def multiply_by_cos(i, batches):
             x_sb, cos_sb, sin_sb = loaded[i]
-            x_tq = x_sb.rearrange("p b (q t) -> p b t q", t=PACK)
-            x_cos = products.tile([P, B, PACK, Q], F32)
-            nc.vector.tensor_tensor(out=x_cos[:], in0=x_tq, in1=by_word_value(cos_sb), op=MULT)
-            return x_cos
-
-        def multiply_by_sin(i, x_cos):
-            x_sb, cos_sb, sin_sb = loaded[i]
-            rot_sin = products.tile([P, B, PACK, Q], F32)
+            x_cos, rot_sin = multiplied[i]
             nc.vector.tensor_tensor(
-                out=rot_sin[:].rearrange("p b t (h q) -> p b t h q", h=2)[:, :, :, ::-1, :],
-                in0=x_sb.rearrange("p b (h q t) -> p b t h q", h=2, t=PACK),
-                in1=sin_sb.rearrange("p (h q t) -> p t h q", h=2, t=PACK)
+                out=x_cos[:, batches],
+                in0=x_sb[:, batches].rearrange("p b (q t) -> p b t q", t=PACK),
+                in1=cos_sb.rearrange("p (q t) -> p t q", t=PACK)
                 .unsqueeze(1)
-                .to_broadcast([P, B, PACK, 2, HALF_Q]),
+                .to_broadcast([P, batches.stop - batches.start, PACK, Q]),
                 op=MULT,
             )
-            multiplied[i] = (x_cos, rot_sin)
+
+        def multiply_by_sin(i, batches):
+            x_sb, cos_sb, sin_sb = loaded[i]
+            x_cos, rot_sin = multiplied[i]
+            nc.vector.tensor_tensor(
+                out=rot_sin[:, batches].rearrange("p b t (h q) -> p b t h q", h=2)[:, :, :, ::-1, :],
+                in0=x_sb[:, batches].rearrange("p b (h q t) -> p b t h q", h=2, t=PACK),
+                in1=sin_sb.rearrange("p (h q t) -> p t h q", h=2, t=PACK)
+                .unsqueeze(1)
+                .to_broadcast([P, batches.stop - batches.start, PACK, 2, HALF_Q]),
+                op=MULT,
+            )
 
         def transpose_and_add(i):
             x_cos, rot_sin = multiplied[i]
@@ -107,40 +112,43 @@ def tile_denseattentiononehead_pa_t_kernel(
                         is_transpose=True, start=False, stop=True,
                     )
 
-        def regroup(i):
-            h_grouped = quantised.tile([P, B, P, PACK], BF16, align_bytes=64)
-            for b in range(B):
-                nc.scalar.copy(
-                    out=h_grouped[:, b, :, :],
-                    in_=transposed[(i, b)][:].rearrange("p t w -> p w t"),
-                )
-            grouped[i] = h_grouped
+        def regroup(i, b, engine_copy):
+            engine_copy(
+                out=grouped[i][:, b, :, :], in_=transposed[(i, b)][:].rearrange("p t w -> p w t")
+            )
 
-        def quantise(i):
+        def quantise(i, batches):
+            h_codes, h_scales = packed[i]
+            tokens = slice(batches.start * P, batches.stop * P)
+            nc.vector.quantize_mx(
+                out=h_codes[:, tokens].bitcast(FP8X4),
+                scales=h_scales[:, tokens],
+                in_=grouped[i][:, batches].rearrange("p b w t -> p (b w t)"),
+            )
+
+        def project(i, acc, b):
+            h_codes, h_scales = packed[i]
+            tokens = slice(b * P, (b + 1) * P)
+            nc.tensor.matmul_mx(
+                out=acc[:],
+                lhsT=h_codes[:, tokens].bitcast(FP8X4),
+                lhsT_scale=h_scales[:, tokens],
+                rhs=w_words[:].bitcast(FP4X4),
+                rhs_scale=w_scales[:],
+                start=True,
+                stop=True,
+            )
+            projected[(i, b)] = acc
+
+        def new_tiles(i):
+            x_cos = products.tile([P, B, PACK, Q], F32)
+            rot_sin = products.tile([P, B, PACK, Q], F32)
+            multiplied[i] = (x_cos, rot_sin)
+            h_grouped = quantised.tile([P, B, P, PACK], BF16, align_bytes=64)
+            grouped[i] = h_grouped
             h_codes = quantised.tile([P, B * P], U32, align_bytes=64)
             h_scales = quantised.tile([P, B * P], U8, align_bytes=64)
-            nc.vector.quantize_mx(
-                out=h_codes[:].bitcast(FP8X4),
-                scales=h_scales[:],
-                in_=grouped[i][:].rearrange("p b w t -> p (b w t)"),
-            )
             packed[i] = (h_codes, h_scales)
-
-        def project(i):
-            h_codes, h_scales = packed[i]
-            for b in range(B):
-                tokens = slice(b * P, (b + 1) * P)
-                acc = psum_out.tile([P, H], F32)
-                nc.tensor.matmul_mx(
-                    out=acc[:],
-                    lhsT=h_codes[:, tokens].bitcast(FP8X4),
-                    lhsT_scale=h_scales[:, tokens],
-                    rhs=w_words[:].bitcast(FP4X4),
-                    rhs_scale=w_scales[:],
-                    start=True,
-                    stop=True,
-                )
-                projected[(i, b)] = acc
 
         def copy_out(i, vector_helps):
             out_sb = results.tile([P, B, H], F32)
@@ -169,26 +177,38 @@ def tile_denseattentiononehead_pa_t_kernel(
 
         for s in range(STEPS):
             negate(s + 1)
-            x_cos = multiply_by_cos(s)
-            if 0 <= s - 2:
-                quantise(s - 2)
-            multiply_by_sin(s, x_cos)
+            new_tiles(s)
+            for part in HALVES if s in (0, STEPS - 1) else (ALL,):
+                multiply_by_cos(s, part)
+                if part.start == 0 and 0 <= s - 2:
+                    quantise(s - 2, ALL)
+                multiply_by_sin(s, part)
             if 0 <= s - 1:
                 transpose_and_add(s - 1)
-                regroup(s - 1)
+                for b in range(B):
+                    regroup(s - 1, b, nc.scalar.copy)
             if 0 <= s - 2:
-                project(s - 2)
+                for b in range(B):
+                    acc = psum_out.tile([P, H], F32)
+                    project(s - 2, acc, b)
                 out_sb = copy_out(s - 2, False)
                 nc.sync.dma_start(out=out_dram[s - 2], in_=out_sb[:])
 
-        quantise(STEPS - 2)
-        transpose_and_add(STEPS - 1)
-        regroup(STEPS - 1)
-        project(STEPS - 2)
-        quantise(STEPS - 1)
-        out_sb = copy_out(STEPS - 2, True)
-        nc.sync.dma_start(out=out_dram[STEPS - 2], in_=out_sb[:])
-        project(STEPS - 1)
-        out_sb = copy_out(STEPS - 1, True)
+        last = STEPS - 1
+        quantise(last - 1, ALL)
+        transpose_and_add(last)
+        for part in HALVES:
+            regroup(last, part.start, nc.scalar.copy)
+            regroup(last, part.start + 1, nc.vector.tensor_copy)
+            quantise(last, part)
         for b in range(B):
-            nc.sync.dma_start(out=out_dram[STEPS - 1][:, b, :], in_=out_sb[:, b, :])
+            acc = psum_out.tile([P, H], F32)
+            project(last - 1, acc, b)
+        for b in range(B):
+            acc = psum_h.tile([P, H], F32, name="h_T")
+            project(last, acc, b)
+        out_sb = copy_out(last - 1, True)
+        nc.sync.dma_start(out=out_dram[last - 1], in_=out_sb[:])
+        out_sb = copy_out(last, True)
+        for b in range(B):
+            nc.sync.dma_start(out=out_dram[last][:, b, :], in_=out_sb[:, b, :])

from contextlib import ExitStack

import concourse.mybir as mybir
from concourse.masks import make_identity

BF16 = mybir.dt.bfloat16
F32 = mybir.dt.float32
I32 = mybir.dt.int32
U8 = mybir.dt.uint8
U32 = mybir.dt.uint32
FP8X4 = mybir.dt.float8_e4m3fn_x4
FP4X4 = mybir.dt.float4_e2m1fn_x4
MULT = mybir.AluOpType.mult

B, L, H = 4, 2048, 512
P = 128
PACK = 4
Q = H // PACK
HALF_Q = Q // 2
STEPS = L // P
CHUNKS = (1, 1, 2, 4, 4, 4)
ALL = slice(0, B)
HALVES = (slice(0, B // 2), slice(B // 2, B))

FLOPS = 2 * B * L * H * H


def tile_denseattentiononehead_pa_t_kernel(
    tc, hidden_states, W_q_words, W_q_scales, cos, sin, out
):
    nc = tc.nc
    x_dram = hidden_states.rearrange("b (p n) j -> p b n j", n=STEPS)
    cos_dram = cos.rearrange("(p n) j -> p n j", n=STEPS)
    sin_dram = sin.rearrange("(p n) j -> p n j", n=STEPS)
    out_dram = out.rearrange("b (p n) o -> n p b o", n=STEPS)

    with ExitStack() as ctx:
        consts = ctx.enter_context(tc.tile_pool(name="consts", bufs=1))
        inputs = ctx.enter_context(tc.tile_pool(name="inputs", bufs=1))
        products = ctx.enter_context(tc.tile_pool(name="products", bufs=3))
        quantised = ctx.enter_context(tc.tile_pool(name="quantised", bufs=3))
        results = ctx.enter_context(tc.tile_pool(name="results", bufs=4))
        psum_h = ctx.enter_context(tc.psum_pool(name="psum_h", bufs=B))
        psum_out = ctx.enter_context(tc.psum_pool(name="psum_out", bufs=B))
        ctx.enter_context(tc.manual_schedule())

        identity = consts.tile([P, P], F32)
        make_identity(nc, identity[:])

        loaded, multiplied, transposed, grouped, packed, projected, chunk_of = (
            {}, {}, {}, {}, {}, {}, {},
        )

        def load(chunk, first, steps):
            rows = slice(first, first + steps)
            x_sb = inputs.tile([P, B, steps, H], BF16, name="x%d" % chunk)
            cos_sb = inputs.tile([P, steps, H], BF16, name="cos%d" % chunk)
            sin_sb = inputs.tile([P, steps, H], BF16, name="sin%d" % chunk)
            sin_low = inputs.tile([P, steps, H // 2], BF16, name="sin_low%d" % chunk)
            early = B // 2 if chunk == 0 else B
            nc.sync.dma_start(out=x_sb[:, 0:early], in_=x_dram[:, 0:early, rows, :])
            nc.sync.dma_start(out=cos_sb[:], in_=cos_dram[:, rows, :])
            nc.sync.dma_start(out=sin_low[:], in_=sin_dram[:, rows, 0 : H // 2])
            nc.sync.dma_start(out=sin_sb[:, :, 0 : H // 2], in_=sin_dram[:, rows, H // 2 : H])
            if early < B:
                nc.sync.dma_start(out=x_sb[:, early:B], in_=x_dram[:, early:B, rows, :])
            for k in range(steps):
                loaded[first + k] = (x_sb[:, :, k, :], cos_sb[:, k, :], sin_sb[:, k, :])
            chunk_of[first] = (sin_sb, sin_low)

        def negate(i):
            if i in chunk_of:
                sin_sb, sin_low = chunk_of[i]
                nc.scalar.mul(out=sin_sb[:, :, H // 2 : H], in_=sin_low[:], mul=-1.0)

        def multiply_by_cos(i, batches):
            x_sb, cos_sb, sin_sb = loaded[i]
            x_cos, rot_sin = multiplied[i]
            nc.vector.tensor_tensor(
                out=x_cos[:, batches],
                in0=x_sb[:, batches].rearrange("p b (q t) -> p b t q", t=PACK),
                in1=cos_sb.rearrange("p (q t) -> p t q", t=PACK)
                .unsqueeze(1)
                .to_broadcast([P, batches.stop - batches.start, PACK, Q]),
                op=MULT,
            )

        def multiply_by_sin(i, batches):
            x_sb, cos_sb, sin_sb = loaded[i]
            x_cos, rot_sin = multiplied[i]
            nc.vector.tensor_tensor(
                out=rot_sin[:, batches].rearrange("p b t (h q) -> p b t h q", h=2)[:, :, :, ::-1, :],
                in0=x_sb[:, batches].rearrange("p b (h q t) -> p b t h q", h=2, t=PACK),
                in1=sin_sb.rearrange("p (h q t) -> p t h q", h=2, t=PACK)
                .unsqueeze(1)
                .to_broadcast([P, batches.stop - batches.start, PACK, 2, HALF_Q]),
                op=MULT,
            )

        def transpose_and_add(i):
            x_cos, rot_sin = multiplied[i]
            for b in range(B):
                h_T = psum_h.tile([P, PACK, P], F32)
                transposed[(i, b)] = h_T
                for t in range(PACK):
                    nc.tensor.matmul(
                        h_T[:, t, :], lhsT=x_cos[:, b, t, :], rhs=identity[:],
                        is_transpose=True, start=True, stop=False,
                    )
                    nc.tensor.matmul(
                        h_T[:, t, :], lhsT=rot_sin[:, b, t, :], rhs=identity[:],
                        is_transpose=True, start=False, stop=True,
                    )

        def regroup(i, b, engine_copy):
            engine_copy(
                out=grouped[i][:, b, :, :], in_=transposed[(i, b)][:].rearrange("p t w -> p w t")
            )

        def quantise(i, batches):
            h_codes, h_scales = packed[i]
            tokens = slice(batches.start * P, batches.stop * P)
            nc.vector.quantize_mx(
                out=h_codes[:, tokens].bitcast(FP8X4),
                scales=h_scales[:, tokens],
                in_=grouped[i][:, batches].rearrange("p b w t -> p (b w t)"),
            )

        def project(i, acc, b):
            h_codes, h_scales = packed[i]
            tokens = slice(b * P, (b + 1) * P)
            nc.tensor.matmul_mx(
                out=acc[:],
                lhsT=h_codes[:, tokens].bitcast(FP8X4),
                lhsT_scale=h_scales[:, tokens],
                rhs=w_words[:].bitcast(FP4X4),
                rhs_scale=w_scales[:],
                start=True,
                stop=True,
            )
            projected[(i, b)] = acc

        def new_tiles(i):
            x_cos = products.tile([P, B, PACK, Q], F32)
            rot_sin = products.tile([P, B, PACK, Q], F32)
            multiplied[i] = (x_cos, rot_sin)
            h_grouped = quantised.tile([P, B, P, PACK], BF16, align_bytes=64)
            grouped[i] = h_grouped
            h_codes = quantised.tile([P, B * P], U32, align_bytes=64)
            h_scales = quantised.tile([P, B * P], U8, align_bytes=64)
            packed[i] = (h_codes, h_scales)

        def copy_out(i, vector_helps):
            out_sb = results.tile([P, B, H], F32)
            for b in range(B):
                if vector_helps and b % 2 == 1:
                    nc.vector.tensor_copy(out=out_sb[:, b, :], in_=projected[(i, b)][:])
                else:
                    nc.scalar.copy(out=out_sb[:, b, :], in_=projected[(i, b)][:])
            return out_sb

        load(0, 0, CHUNKS[0])

        w_words = consts.tile([P, 2 * H], U8, align_bytes=64)
        nc.sync.dma_start(out=w_words[:].bitcast(I32), in_=W_q_words[0].bitcast(I32))
        w_scales = consts.tile([P, H], U8, align_bytes=64)
        nc.vector.memset(w_scales[:].bitcast(I32), 0)
        for quadrant in range(4):
            nc.sync.dma_start(
                out=w_scales[32 * quadrant : 32 * quadrant + 4, :].bitcast(I32),
                in_=W_q_scales[0, 4 * quadrant : 4 * quadrant + 4, :].bitcast(I32),
            )

        for chunk in range(1, len(CHUNKS)):
            load(chunk, sum(CHUNKS[:chunk]), CHUNKS[chunk])
        negate(0)

        for s in range(STEPS):
            negate(s + 1)
            new_tiles(s)
            for part in HALVES if s in (0, STEPS - 1) else (ALL,):
                multiply_by_cos(s, part)
                if part.start == 0 and 0 <= s - 2:
                    quantise(s - 2, ALL)
                multiply_by_sin(s, part)
            if 0 <= s - 1:
                transpose_and_add(s - 1)
                for b in range(B):
                    regroup(s - 1, b, nc.scalar.copy)
            if 0 <= s - 2:
                for b in range(B):
                    acc = psum_out.tile([P, H], F32)
                    project(s - 2, acc, b)
                out_sb = copy_out(s - 2, False)
                nc.sync.dma_start(out=out_dram[s - 2], in_=out_sb[:])

        last = STEPS - 1
        quantise(last - 1, ALL)
        transpose_and_add(last)
        for part in HALVES:
            regroup(last, part.start, nc.scalar.copy)
            regroup(last, part.start + 1, nc.vector.tensor_copy)
            quantise(last, part)
        for b in range(B):
            acc = psum_out.tile([P, H], F32)
            project(last - 1, acc, b)
        for b in range(B):
            acc = psum_h.tile([P, H], F32, name="h_T")
            project(last, acc, b)
        out_sb = copy_out(last - 1, True)
        nc.sync.dma_start(out=out_dram[last - 1], in_=out_sb[:])
        out_sb = copy_out(last, True)
        for b in range(B):
            nc.sync.dma_start(out=out_dram[last][:, b, :], in_=out_sb[:, b, :])
